import numpy as np
import ml_dtypes


def mxq(x, axis, fmt="e4m3"):
    dtype, down = {"e4m3": (ml_dtypes.float8_e4m3fn, 7), "e5m2": (ml_dtypes.float8_e5m2, 14)}[fmt]
    v = np.moveaxis(np.asarray(x, np.float32).astype(ml_dtypes.bfloat16).astype(np.float64), axis, -1)
    blocks = v.reshape(v.shape[:-1] + (-1, 32))
    amax = np.abs(blocks).max(-1, keepdims=True)
    byte = np.maximum(np.where(amax > 0, np.frexp(amax)[1] - 1 + 127, 0) - down, 1)
    scale = np.exp2(byte - 127.0)
    codes = (blocks / scale).astype(np.float32).astype(dtype).astype(np.float64)
    return np.moveaxis((codes * scale).reshape(v.shape), -1, axis)


WIDE = False


def mx_kscale(k):
    if not WIDE:
        return np.ones(k)
    levels = np.array([10, -10, 5, -5, 0])
    a = np.random.permutation(np.resize(levels, k // 512 * 4)).reshape(k // 512, 4)
    idx = np.arange(k)
    return np.exp2(a[idx // 512, idx % 128 // 32])


BF16 = ml_dtypes.bfloat16


def bf(x):
    return np.asarray(x, np.float32).astype(BF16)


def f64(x):
    return np.asarray(x).astype(np.float64)


B, H, W, C, NH, WS, SH, HID = 2, 48, 48, 1024, 16, 16, 7, 512
HD = C // NH
WW = WS * WS
PT, PL = WS - SH, WS - SH
HP, WP = H + WS, W + WS
NWH, NWW = HP // WS, WP // WS
NWIN = B * NWH * NWW
EPS = 1e-5
ERF_CLIP, ERF_TERMS = 6.0, 100


def erf(z):
    z = np.clip(z, -ERF_CLIP, ERF_CLIP)
    zz = 2.0 * z * z
    term = z.copy()
    total = z.copy()
    for n in range(1, ERF_TERMS):
        term = term * zz / (2.0 * n + 1.0)
        total = total + term
    return 2.0 / np.sqrt(np.pi) * np.exp(-z * z) * total


def gelu(v):
    return 0.5 * v * (1.0 + erf(v / np.sqrt(2.0)))


def layer_norm(x, g, b):
    m = x.mean(-1, keepdims=True)
    v = ((x - m) ** 2).mean(-1, keepdims=True)
    return (x - m) / np.sqrt(v + EPS) * g + b


def setup_inputs():
    r = np.random.standard_normal
    s = mx_kscale(C)
    return {
        "h_pad": bf(r((B, HP, WP, C)) * 0.7),
        "x": bf(r((B, H * W, C))),
        "sw": bf(r((NH, WW, WW)) / np.sqrt(WW)),
        "sb": bf(r((NH, WW)) * 0.3),
        "g2": bf((1.0 + 0.2 * r(C)) * s),
        "b2": bf(0.2 * r(C) * s),
        "w1": bf(r((C, HID)) / np.sqrt(C) / s[:, None]),
        "bb1": bf(r(HID) * 0.3),
    }


def reference(h_pad, x, sw, sb, g2, b2, w1, bb1):
    hw = (f64(h_pad).reshape(B, NWH, WS, NWW, WS, NH, HD)
          .transpose(5, 2, 4, 0, 1, 3, 6)
          .reshape(NH, WW, NWIN * HD))
    m = f64(sw) @ hw + f64(sb)[:, :, None]
    m = (m.reshape(NH, WS, WS, B, NWH, NWW, HD)
          .transpose(3, 4, 1, 5, 2, 0, 6)
          .reshape(B, HP, WP, C))
    m = m[:, PT:PT + H, PL:PL + W, :].reshape(B, H * W, C)
    x1 = f64(x) + m
    h2 = layer_norm(x1, f64(g2), f64(b2))
    a = (mxq(h2, 2, "e4m3") @ mxq(f64(w1), 0, "e4m3")) + f64(bb1)
    return gelu(a)

@@ -1,0 +1,406 @@
+from contextlib import ExitStack
+
+import concourse.mybir as mybir
+from concourse.masks import make_identity
+
+F32 = mybir.dt.float32
+BF16 = mybir.dt.bfloat16
+I32 = mybir.dt.int32
+U32 = mybir.dt.uint32
+U8 = mybir.dt.uint8
+FP8X4 = mybir.dt.float8_e4m3fn_x4
+ALU = mybir.AluOpType
+ACT = mybir.ActivationFunctionType
+
+P = 128
+IMAGES = 2
+WS = 16
+WINDOWS = 4
+CROP = 9
+MAP = 48
+C = 1024
+HEADS = 16
+HD = C // HEADS
+HID = 512
+EPS = 1e-5
+ROWS = 8
+SEAM = CROP + MAP - WS * (WINDOWS - 1)
+LEFT = SEAM * ROWS
+UNITS = 6
+PACK = 4
+K_PASS = P * PACK
+PASSES = C // K_PASS
+BLOCKS = C // P
+STRIP = ROWS * MAP
+STRIP_TILES = STRIP // P
+MARGIN = 16
+SPLIT = LEFT + P
+
+FLOPS = 2 * HEADS * (WS * WS) * (WS * WS) * (IMAGES * WINDOWS * WINDOWS * HD) + 2 * IMAGES * MAP * MAP * C * HID
+
+
+def tile_swinmlpblock_pa_t_kernel(tc, h_pad, x, sw, sb, g2, b2, w1, bb1, out):
+    nc = tc.nc
+    with ExitStack() as ctx:
+        const = ctx.enter_context(tc.tile_pool(name="const", bufs=1))
+        win_pool = ctx.enter_context(tc.tile_pool(name="windows", bufs=2))
+        x_pool = ctx.enter_context(tc.tile_pool(name="x", bufs=2))
+        x1_pool = ctx.enter_context(tc.tile_pool(name="x1", bufs=2))
+        small = ctx.enter_context(tc.tile_pool(name="small", bufs=4))
+        plane_pool = ctx.enter_context(tc.tile_pool(name="planes", bufs=2))
+        group_pool = ctx.enter_context(tc.tile_pool(name="grouped", bufs=2))
+        code_pool = ctx.enter_context(tc.tile_pool(name="codes", bufs=2))
+        act_pool = ctx.enter_context(tc.tile_pool(name="act", bufs=3))
+        psum = ctx.enter_context(tc.psum_pool(name="psum", bufs=8))
+
+        win_view = h_pad.rearrange("b (wr r) (wc k q) c -> b wr wc r k (q c)", r=WS, wc=WINDOWS, k=WS // 2, q=2)
+        x_view = x.rearrange("b (y w) c -> b w y c", w=MAP)
+
+        ident_f = const.tile([P, P], F32)
+        make_identity(nc, ident_f[:])
+        ident_b = const.tile([P, P], BF16)
+        make_identity(nc, ident_b[:])
+        minus_half = const.tile([P, 2], F32)
+        nc.vector.memset(minus_half[:], -0.5)
+
+        def load_windows(wrow):
+            inner = win_pool.tile([P, 4, 2, C], BF16, tag="inner")
+            last = win_pool.tile([P, 2, 2, C], BF16, tag="last")
+            first = win_pool.tile([P, 2, 2, C], BF16, tag="first")
+            for b in range(IMAGES):
+                for wcol in (1, 2):
+                    nc.sync.dma_start(
+                        out=inner[:, 2 * b + wcol - 1, :, :].rearrange("p q c -> p (q c)"),
+                        in_=win_view[b, wrow, wcol],
+                    )
+            for b in range(IMAGES):
+                nc.sync.dma_start(
+                    out=last[:, b, :, :].rearrange("p q c -> p (q c)"), in_=win_view[b, wrow, WINDOWS - 1]
+                )
+                nc.sync.dma_start(out=first[:, b, :, :].rearrange("p q c -> p (q c)"), in_=win_view[b, wrow, 0])
+            return inner, last, first
+
+        def load_x(y0, y_last):
+            x_sb = x_pool.tile([P, UNITS, C], BF16, tag="x")
+            for b in range(IMAGES):
+                pieces = [(0, P, 2 * b + wcol - 1, WS * wcol - CROP) for wcol in (1, 2)]
+                pieces.append((0, LEFT, 4 + b, MAP - SEAM))
+                pieces.append((LEFT, P, 4 + b, 0))
+                for p0, p1, n, w0 in pieces:
+                    w1_ = w0 + (p1 - p0) // ROWS
+                    nc.sync.dma_start(out=x_sb[p0:p1, n, :], in_=x_view[b, w0:w1_, y0 : y0 + ROWS, :])
+                    if y_last != y0 + ROWS - 1:
+                        nc.sync.dma_start(out=x_sb[p0 + ROWS - 1 : p1 : ROWS, n, :], in_=x_view[b, w0:w1_, y_last, :])
+            return x_sb
+
+        sw_nat = x1_pool.tile([P, 2, HEADS, WS * WS], BF16, tag="x1")
+        sw_view = sw.rearrange("h (t p) j -> t p h j", t=2)
+        nc.sync.dma_start(out=sw_nat[:, 0], in_=sw_view[0])
+        windows = load_windows(1)
+        x_next = load_x(WS - CROP, WS - CROP + ROWS - 1)
+        nc.sync.dma_start(out=sw_nat[:, 1], in_=sw_view[1])
+
+        vec_rows = act_pool.tile([P, P], BF16, tag="act")
+        nc.vector.memset(vec_rows[:].bitcast(I32), 0)
+        nc.scalar.dma_start(out=vec_rows[0:BLOCKS, :], in_=g2.rearrange("(k p) -> k p", p=P))
+        nc.scalar.dma_start(out=vec_rows[BLOCKS : 2 * BLOCKS, :], in_=b2.rearrange("(k p) -> k p", p=P))
+        sb_rows = act_pool.tile([P, 2 * P], BF16, tag="act")
+        nc.vector.memset(sb_rows[:].bitcast(I32), 0)
+        nc.scalar.dma_start(out=sb_rows[0:HEADS, :], in_=sb)
+        bias_bc = const.tile([P, HID], BF16)
+        nc.scalar.dma_start(out=bias_bc[:], in_=bb1.partition_broadcast(P))
+        sb_perm = act_pool.tile([P, 3, WS, ROWS], BF16, tag="act")
+        nc.vector.tensor_copy(
+            out=sb_perm[:, 0:2, :, :], in_=sb_rows[:].rearrange("p (t r c) -> p t c r", t=2, r=ROWS, c=WS)
+        )
+        nc.vector.tensor_copy(out=sb_perm[:, 2, :, 0 : ROWS - 1], in_=sb_perm[:, 1, :, 1:ROWS])
+        nc.vector.tensor_copy(out=sb_perm[:, 2, :, ROWS - 1 : ROWS], in_=sb_perm[:, 1, :, 0:1])
+        vec_ps = psum.tile([P, 4, P], BF16, tag="bank")
+        nc.tensor.transpose(out=vec_ps[:, 0, :], in_=vec_rows[:], identity=ident_b[:])
+        for i in range(3):
+            nc.tensor.transpose(
+                out=vec_ps[:, 1 + i, :], in_=sb_perm[:, i, :, :].rearrange("p c r -> p (c r)"), identity=ident_b[:]
+            )
+        gain_shift = const.tile([P, 2 * BLOCKS], F32)
+        nc.vector.tensor_copy(out=gain_shift[:], in_=vec_ps[:, 0, 0 : 2 * BLOCKS])
+        sb_col = const.tile([P, 3, HEADS], F32)
+        nc.vector.tensor_copy(out=sb_col[:], in_=vec_ps[:, 1:4, 0:HEADS])
+
+        n_blocks = 2 * HEADS
+        whole = [const.tile([P, 2 * MARGIN + n_blocks * P], BF16, name="whole%d" % half) for half in range(2)]
+        split = [const.tile([P, 2 * MARGIN + n_blocks * SPLIT], BF16, name="split%d" % half) for half in range(2)]
+        orphan = const.tile([P, 2 * MARGIN + n_blocks * SPLIT], BF16)
+        for t in whole:
+            nc.vector.memset(t[:, 0:MARGIN].bitcast(I32), 0)
+            nc.vector.memset(t[:, MARGIN + n_blocks * P :].bitcast(I32), 0)
+        for t in split + [orphan]:
+            nc.vector.memset(t[:].bitcast(I32), 0)
+
+        def by_block(t, width):
+            return t[:, MARGIN : MARGIN + n_blocks * width].rearrange("p (n m) -> p n m", m=width)
+
+        def prepare_weights(half):
+            for quad in range(HEADS // 4):
+                sw_ps = psum.tile([P, 8, P], BF16, tag="bank")
+                for i in range(8):
+                    h, q = 4 * quad + i // 2, i % 2
+                    nc.tensor.transpose(
+                        out=sw_ps[:, i, :],
+                        in_=sw_nat[:, half, h, :].rearrange("p (k q) -> p q k", q=2)[:, q, :],
+                        identity=ident_b[:],
+                    )
+                dst = by_block(whole[half], P)[:, 8 * quad : 8 * (quad + 1), :].rearrange(
+                    "p n (c r) -> p n c r", c=WS, r=ROWS
+                )
+                src = sw_ps[:].rearrange("p n (r c) -> p n c r", r=ROWS, c=WS)
+                if quad % 2 == 0:
+                    nc.vector.tensor_copy(out=dst, in_=src)
+                else:
+                    nc.scalar.copy(out=dst, in_=src)
+            nc.vector.tensor_copy(out=by_block(split[half], SPLIT)[:, :, 0:LEFT], in_=by_block(whole[half], P)[:, :, 0:LEFT])
+            nc.vector.tensor_copy(
+                out=by_block(split[half], SPLIT)[:, :, 2 * LEFT : SPLIT], in_=by_block(whole[half], P)[:, :, LEFT:P]
+            )
+
+        def first_rows(t, width, m0, m1):
+            return by_block(t, width)[:, :, m0:m1].rearrange("p n (c r) -> p n c r", r=ROWS)[:, :, :, 0:1]
+
+        def prepare_seam_weights():
+            nc.gpsimd.tensor_copy(out=first_rows(orphan, SPLIT, 0, LEFT), in_=first_rows(split[1], SPLIT, 0, LEFT))
+            nc.gpsimd.tensor_copy(
+                out=first_rows(orphan, SPLIT, 2 * LEFT, SPLIT), in_=first_rows(split[1], SPLIT, 2 * LEFT, SPLIT)
+            )
+            nc.gpsimd.memset(first_rows(whole[1], P, 0, P), 0.0)
+            nc.gpsimd.memset(first_rows(split[1], SPLIT, 0, LEFT), 0.0)
+            nc.gpsimd.memset(first_rows(split[1], SPLIT, 2 * LEFT, SPLIT), 0.0)
+
+        prepare_weights(0)
+
+        w1_codes = const.tile([P, PASSES, HID], U32, align_bytes=64)
+        w1_scales = const.tile([P, PASSES, HID], U8, align_bytes=64)
+
+        def prepare_w1():
+            w1_view = w1.rearrange("(g t p) n -> g p t n", g=PASSES, t=PACK)
+            for g in range(PASSES):
+                raw = plane_pool.tile([P, PACK, HID], BF16, tag="planes")
+                nc.sync.dma_start(out=raw[:], in_=w1_view[g])
+                grouped = group_pool.tile([P, HID, PACK], BF16, tag="grouped", align_bytes=64)
+                nc.vector.tensor_copy(out=grouped[:], in_=raw[:].rearrange("p t n -> p n t"))
+                nc.vector.quantize_mx(
+                    out=w1_codes[:, g, :].bitcast(FP8X4),
+                    scales=w1_scales[:, g, :],
+                    in_=grouped[:].rearrange("p n t -> p (n t)"),
+                )
+
+        def accumulate(acc, terms):
+            for i, (weights, moving) in enumerate(terms):
+                nc.tensor.matmul(out=acc, lhsT=weights, rhs=moving, start=(i == 0), stop=(i == len(terms) - 1))
+
+        def mix(sources, sb_index, x_sb, x1, heads):
+            for h in heads:
+                cols = slice(HD * h, HD * (h + 1))
+                inner_terms, seam_terms = [], []
+                for (inner, last, first), whole_w, split_w, start in sources:
+                    for q in range(2):
+                        n = 2 * h + q
+                        s0 = MARGIN + SPLIT * n + start
+                        left_w = split_w[:, s0 : s0 + P]
+                        right_w = split_w[:, s0 + LEFT : s0 + LEFT + P]
+                        if whole_w is None:
+                            inner_terms.append((left_w, inner[:, :, q, cols]))
+                            inner_terms.append((right_w, inner[:, :, q, cols]))
+                        else:
+                            w0 = MARGIN + P * n + start
+                            inner_terms.append((whole_w[:, w0 : w0 + P], inner[:, :, q, cols]))
+                        seam_terms.append((left_w, last[:, :, q, cols]))
+                        seam_terms.append((right_w, first[:, :, q, cols]))
+                acc = psum.tile([P, UNITS, HD], F32, tag="bank")
+                accumulate(acc[:, 0:4, :], inner_terms)
+                accumulate(acc[:, 4:6, :], seam_terms)
+                nc.vector.scalar_tensor_tensor(
+                    out=x1[:, :, cols],
+                    in0=acc[:],
+                    scalar=sb_col[:, sb_index, h : h + 1],
+                    in1=x_sb[:, :, cols],
+                    op0=ALU.add,
+                    op1=ALU.add,
+                )
+
+        def statistics(x1, x_sb, b):
+            seam, inner = 4 + b, (2 * b, 2 * b + 1)
+            stats = small.tile([P, 2, 6], F32, tag="stats")
+            for i in range(2):
+                nc.vector.bn_stats(out=stats[:, i, :], in_=x1[:, seam, 512 * i : 512 * (i + 1)])
+            mean_var = small.tile([P, 2], F32, tag="mean_var")
+            nc.vector.bn_aggr(out=mean_var[:], in_=stats[:])
+            sums = small.tile([P, 2], F32, tag="sums")
+            for j, n in enumerate(inner):
+                nc.scalar.activation(out=x_sb[:, n, :], in_=x1[:, n, :], func=ACT.Identity, accum_out=sums[:, j : j + 1])
+            neg_mean = small.tile([P, 2], F32, tag="neg_mean")
+            nc.scalar.mul(out=neg_mean[:], in_=sums[:], mul=-1.0 / C)
+            squares = small.tile([P, 2], F32, tag="squares")
+            for j, n in enumerate(inner):
+                nc.scalar.activation(
+                    out=x_sb[:, n, :],
+                    in_=x1[:, n, :],
+                    func=ACT.Square,
+                    bias=neg_mean[:, j : j + 1],
+                    accum_out=squares[:, j : j + 1],
+                )
+            return mean_var, neg_mean, squares
+
+        def scale(x1, b, mean_var, neg_mean, squares):
+            seam, inner = 4 + b, (2 * b, 2 * b + 1)
+            seam_scalars = small.tile([P, 2], F32, tag="seam_scalars")
+            nc.gpsimd.tensor_scalar(
+                out=seam_scalars[:, 0:1], in0=mean_var[:, 0:1], scalar1=-1.0, scalar2=0.0, op0=ALU.mult, op1=ALU.add
+            )
+            nc.gpsimd.tensor_scalar(
+                out=seam_scalars[:, 1:2], in0=mean_var[:, 1:2], scalar1=1.0, scalar2=EPS, op0=ALU.mult, op1=ALU.add
+            )
+            nc.gpsimd.tensor_tensor(
+                out=seam_scalars[:, 1:2], in0=seam_scalars[:, 1:2], in1=minus_half[:, 0:1], op=ALU.pow
+            )
+            rstd = small.tile([P, 2], F32, tag="rstd")
+            nc.gpsimd.tensor_scalar(
+                out=rstd[:], in0=squares[:], scalar1=1.0 / C, scalar2=EPS, op0=ALU.mult, op1=ALU.add
+            )
+            nc.gpsimd.tensor_tensor(out=rstd[:], in0=rstd[:], in1=minus_half[:], op=ALU.pow)
+            nc.vector.tensor_scalar(
+                out=x1[:, seam, :],
+                in0=x1[:, seam, :],
+                scalar1=seam_scalars[:, 0:1],
+                scalar2=seam_scalars[:, 1:2],
+                op0=ALU.add,
+                op1=ALU.mult,
+            )
+            for j, n in enumerate(inner):
+                nc.vector.tensor_scalar(
+                    out=x1[:, n, :],
+                    in0=x1[:, n, :],
+                    scalar1=neg_mean[:, j : j + 1],
+                    scalar2=rstd[:, j : j + 1],
+                    op0=ALU.add,
+                    op1=ALU.mult,
+                )
+
+        def flip(x1, b):
+            planes = plane_pool.tile([P, BLOCKS, 3 * P], BF16, tag="planes")
+            for k in range(BLOCKS):
+                turned = psum.tile([P, 3, P], F32, tag="bank")
+                for slot, n in enumerate((4 + b, 2 * b, 2 * b + 1)):
+                    nc.tensor.transpose(out=turned[:, slot, :], in_=x1[:, n, P * k : P * (k + 1)], identity=ident_f[:])
+                nc.scalar.activation(
+                    out=planes[:, k, :],
+                    in_=turned[:].rearrange("p s m -> p (s m)"),
+                    func=ACT.Identity,
+                    scale=gain_shift[:, k : k + 1],
+                    bias=gain_shift[:, BLOCKS + k : BLOCKS + k + 1],
+                )
+            return planes
+
+        def pack(planes):
+            grouped = group_pool.tile([P, PASSES, STRIP, PACK], BF16, tag="grouped", align_bytes=64)
+            codes = code_pool.tile([P, PASSES, STRIP], U32, tag="codes", align_bytes=64)
+            scales = code_pool.tile([P, PASSES, STRIP], U8, tag="scales", align_bytes=64)
+            for g in range(PASSES):
+                src = planes[:, PACK * g : PACK * (g + 1), :].rearrange("p t (w r) -> p r w t", w=MAP, r=ROWS)
+                dst = grouped[:, g, :, :].rearrange("p (r w) t -> p r w t", r=ROWS, w=MAP)
+                nc.vector.tensor_copy(out=dst[:, :, 0 : MAP - SEAM, :], in_=src[:, :, SEAM:MAP, :])
+                nc.vector.tensor_copy(out=dst[:, :, MAP - SEAM : MAP, :], in_=src[:, :, 0:SEAM, :])
+            for g in range(PASSES):
+                for m in range(STRIP_TILES):
+                    nc.vector.quantize_mx(
+                        out=codes[:, g, P * m : P * (m + 1)].bitcast(FP8X4),
+                        scales=scales[:, g, P * m : P * (m + 1)],
+                        in_=grouped[:, g, P * m : P * (m + 1), :].rearrange("p a t -> p (a t)"),
+                    )
+            return codes, scales
+
+        def project(codes, scales, b, y0, y_last):
+            for m in range(STRIP_TILES):
+                acc = psum.tile([P, HID], F32, tag="bank")
+                for g in range(PASSES):
+                    nc.tensor.matmul_mx(
+                        out=acc[:],
+                        lhsT=codes[:, g, P * m : P * (m + 1)].bitcast(FP8X4),
+                        lhsT_scale=scales[:, g, P * m : P * (m + 1)],
+                        rhs=w1_codes[:, g, :].bitcast(FP8X4),
+                        rhs_scale=w1_scales[:, g, :],
+                        start=(g == 0),
+                        stop=(g == PASSES - 1),
+                    )
+                act = act_pool.tile([P, HID], F32, tag="act")
+                nc.vector.tensor_tensor(out=act[:], in0=acc[:], in1=bias_bc[:], op=ALU.add)
+                nc.scalar.activation(out=act[:], in_=act[:], func=ACT.Gelu)
+                row = y0 * MAP + P * m
+                head = P if y_last == y0 + ROWS - 1 else min(P * (m + 1), STRIP - MAP) - P * m
+                nc.scalar.dma_start(out=out[b, row : row + head, :], in_=act[0:head, :])
+                if head < P:
+                    nc.scalar.dma_start(out=out[b, y_last * MAP : (y_last + 1) * MAP, :], in_=act[head:P, :])
+
+        stages = []
+        for wrow in (1, 2, 3):
+            for half in range(2):
+                y0 = WS * wrow + ROWS * half - CROP
+                if y0 + ROWS <= MAP:
+                    stages.append(((wrow,), half, y0, y0 + ROWS - 1))
+        stages.append(((0, WINDOWS - 1), 2, 0, MAP - 1))
+
+        last_second_half = max(i for i, stage in enumerate(stages) if stage[1] == 1)
+        n_stages = len(stages)
+
+        def live(i):
+            return 0 <= i < n_stages
+
+        def sources_of(i):
+            wrows, half = stages[i][0], stages[i][1]
+            if half < 2:
+                return [(held[wrows[0]], whole[half], split[half], 0)]
+            return [(held[wrows[0]], whole[1], split[1], 1), (held[wrows[1]], None, orphan, 1 - ROWS)]
+
+        held = {1: windows}
+        x_of, x1_of, stats_of, planes_of, codes_of = {0: x_next}, {}, {}, {}, {}
+        runs = (range(0, 8), range(8, 12), range(12, 14), range(14, 16))
+        with tc.manual_schedule():
+            for fresh in range(n_stages + 2):
+                ripe, late = fresh - 1, fresh - 2
+                if live(fresh):
+                    x1_of[fresh] = x1_pool.tile([P, UNITS, C], F32, tag="x1", name="x1")
+
+                def mix_run(k):
+                    if live(fresh):
+                        mix(sources_of(fresh), stages[fresh][1], x_of[fresh], x1_of[fresh], runs[k])
+
+                if live(ripe):
+                    for b in range(IMAGES):
+                        stats_of[ripe, b] = statistics(x1_of[ripe], x_of[ripe], b)
+                if live(fresh + 1):
+                    x_of[fresh + 1] = load_x(stages[fresh + 1][2], stages[fresh + 1][3])
+                if live(fresh + 2):
+                    for wrow in stages[fresh + 2][0]:
+                        if wrow not in held:
+                            held[wrow] = load_windows(wrow)
+                if live(late):
+                    codes_of[late, 1] = pack(planes_of[late, 1])
+                mix_run(0)
+                if live(late):
+                    project(codes_of[late, 1][0], codes_of[late, 1][1], 1, stages[late][2], stages[late][3])
+                if live(ripe):
+                    scale(x1_of[ripe], 0, *stats_of[ripe, 0])
+                mix_run(1)
+                if live(ripe):
+                    planes_of[ripe, 0] = flip(x1_of[ripe], 0)
+                    scale(x1_of[ripe], 1, *stats_of[ripe, 1])
+                mix_run(2)
+                if live(ripe):
+                    planes_of[ripe, 1] = flip(x1_of[ripe], 1)
+                    codes_of[ripe, 0] = pack(planes_of[ripe, 0])
+                mix_run(3)
+                if live(ripe):
+                    project(codes_of[ripe, 0][0], codes_of[ripe, 0][1], 0, stages[ripe][2], stages[ripe][3])
+                if fresh == 0:
+                    prepare_weights(1)
+                    prepare_w1()
+                if fresh == last_second_half:
+                    prepare_seam_weights()

@@ -60,6 +60,8 @@ def tile_swinmlpblock_pa_t_kernel(tc, h_pad, x, sw, sb, g2, b2, w1, bb1, out):
         make_identity(nc, ident_f[:])
         ident_b = const.tile([P, P], BF16)
         make_identity(nc, ident_b[:])
+        by_rows = const.tile([P, ROWS, WS], F32)
+        nc.vector.tensor_copy(out=by_rows[:], in_=ident_f[:].rearrange("p (c r) -> p r c", c=WS, r=ROWS))
         minus_half = const.tile([P, 2], F32)
         nc.vector.memset(minus_half[:], -0.5)
 
@@ -287,12 +289,16 @@ def tile_swinmlpblock_pa_t_kernel(tc, h_pad, x, sw, sb, g2, b2, w1, bb1, out):
         def flip(x1, b):
             planes = plane_pool.tile([P, BLOCKS, 3 * P], BF16, tag="planes")
             for k in range(BLOCKS):
-                turned = psum.tile([P, 3, P], F32, tag="bank")
+                turned = psum.tile([P, ROWS, MAP], F32, tag="bank")
                 for slot, n in enumerate((4 + b, 2 * b, 2 * b + 1)):
-                    nc.tensor.transpose(out=turned[:, slot, :], in_=x1[:, n, P * k : P * (k + 1)], identity=ident_f[:])
+                    nc.tensor.transpose(
+                        out=turned[:, :, WS * slot : WS * (slot + 1)],
+                        in_=x1[:, n, P * k : P * (k + 1)],
+                        identity=by_rows[:],
+                    )
                 nc.scalar.activation(
                     out=planes[:, k, :],
-                    in_=turned[:].rearrange("p s m -> p (s m)"),
+                    in_=turned[:].rearrange("p r w -> p (r w)"),
                     func=ACT.Identity,
                     scale=gain_shift[:, k : k + 1],
                     bias=gain_shift[:, BLOCKS + k : BLOCKS + k + 1],
@@ -304,7 +310,7 @@ def tile_swinmlpblock_pa_t_kernel(tc, h_pad, x, sw, sb, g2, b2, w1, bb1, out):
             codes = code_pool.tile([P, PASSES, STRIP], U32, tag="codes", align_bytes=64)
             scales = code_pool.tile([P, PASSES, STRIP], U8, tag="scales", align_bytes=64)
             for g in range(PASSES):
-                src = planes[:, PACK * g : PACK * (g + 1), :].rearrange("p t (w r) -> p r w t", w=MAP, r=ROWS)
+                src = planes[:, PACK * g : PACK * (g + 1), :].rearrange("p t (r w) -> p r w t", r=ROWS, w=MAP)
                 dst = grouped[:, g, :, :].rearrange("p (r w) t -> p r w t", r=ROWS, w=MAP)
                 nc.vector.tensor_copy(out=dst[:, :, 0 : MAP - SEAM, :], in_=src[:, :, SEAM:MAP, :])
                 nc.vector.tensor_copy(out=dst[:, :, MAP - SEAM : MAP, :], in_=src[:, :, 0:SEAM, :])

@@ -341,9 +341,9 @@ def tile_swinmlpblock_pa_t_kernel(tc, h_pad, x, sw, sb, g2, b2, w1, bb1, out):
                 nc.scalar.activation(out=act[:], in_=act[:], func=ACT.Gelu)
                 row = y0 * MAP + P * m
                 head = P if y_last == y0 + ROWS - 1 else min(P * (m + 1), STRIP - MAP) - P * m
-                nc.scalar.dma_start(out=out[b, row : row + head, :], in_=act[0:head, :])
+                nc.sync.dma_start(out=out[b, row : row + head, :], in_=act[0:head, :])
                 if head < P:
-                    nc.scalar.dma_start(out=out[b, y_last * MAP : (y_last + 1) * MAP, :], in_=act[head:P, :])
+                    nc.sync.dma_start(out=out[b, y_last * MAP : (y_last + 1) * MAP, :], in_=act[head:P, :])
 
         stages = []
         for wrow in (1, 2, 3):
@@ -381,17 +381,17 @@ def tile_swinmlpblock_pa_t_kernel(tc, h_pad, x, sw, sb, g2, b2, w1, bb1, out):
                 if live(ripe):
                     for b in range(IMAGES):
                         stats_of[ripe, b] = statistics(x1_of[ripe], x_of[ripe], b)
+                if live(late):
+                    codes_of[late, 1] = pack(planes_of[late, 1])
+                mix_run(0)
+                if live(late):
+                    project(codes_of[late, 1][0], codes_of[late, 1][1], 1, stages[late][2], stages[late][3])
                 if live(fresh + 1):
                     x_of[fresh + 1] = load_x(stages[fresh + 1][2], stages[fresh + 1][3])
                 if live(fresh + 2):
                     for wrow in stages[fresh + 2][0]:
                         if wrow not in held:
                             held[wrow] = load_windows(wrow)
-                if live(late):
-                    codes_of[late, 1] = pack(planes_of[late, 1])
-                mix_run(0)
-                if live(late):
-                    project(codes_of[late, 1][0], codes_of[late, 1][1], 1, stages[late][2], stages[late][3])
                 if live(ripe):
                     scale(x1_of[ripe], 0, *stats_of[ripe, 0])
                 mix_run(1)

@@ -64,6 +64,8 @@ def tile_swinmlpblock_pa_t_kernel(tc, h_pad, x, sw, sb, g2, b2, w1, bb1, out):
         nc.vector.tensor_copy(out=by_rows[:], in_=ident_f[:].rearrange("p (c r) -> p r c", c=WS, r=ROWS))
         minus_half = const.tile([P, 2], F32)
         nc.vector.memset(minus_half[:], -0.5)
+        eps_col = const.tile([P, 1], F32)
+        nc.vector.memset(eps_col[:], EPS)
 
         def load_windows(wrow):
             inner = win_pool.tile([P, 4, 2, C], BF16, tag="inner")
@@ -168,13 +170,13 @@ def tile_swinmlpblock_pa_t_kernel(tc, h_pad, x, sw, sb, g2, b2, w1, bb1, out):
             return by_block(t, width)[:, :, m0:m1].rearrange("p n (c r) -> p n c r", r=ROWS)[:, :, :, 0:1]
 
         def prepare_seam_weights():
-            nc.gpsimd.tensor_copy(out=first_rows(orphan, SPLIT, 0, LEFT), in_=first_rows(split[1], SPLIT, 0, LEFT))
-            nc.gpsimd.tensor_copy(
+            nc.vector.tensor_copy(out=first_rows(orphan, SPLIT, 0, LEFT), in_=first_rows(split[1], SPLIT, 0, LEFT))
+            nc.vector.tensor_copy(
                 out=first_rows(orphan, SPLIT, 2 * LEFT, SPLIT), in_=first_rows(split[1], SPLIT, 2 * LEFT, SPLIT)
             )
-            nc.gpsimd.memset(first_rows(whole[1], P, 0, P), 0.0)
-            nc.gpsimd.memset(first_rows(split[1], SPLIT, 0, LEFT), 0.0)
-            nc.gpsimd.memset(first_rows(split[1], SPLIT, 2 * LEFT, SPLIT), 0.0)
+            nc.vector.memset(first_rows(whole[1], P, 0, P), 0.0)
+            nc.vector.memset(first_rows(split[1], SPLIT, 0, LEFT), 0.0)
+            nc.vector.memset(first_rows(split[1], SPLIT, 2 * LEFT, SPLIT), 0.0)
 
         prepare_weights(0)
 
@@ -235,6 +237,11 @@ def tile_swinmlpblock_pa_t_kernel(tc, h_pad, x, sw, sb, g2, b2, w1, bb1, out):
                 nc.vector.bn_stats(out=stats[:, i, :], in_=x1[:, seam, 512 * i : 512 * (i + 1)])
             mean_var = small.tile([P, 2], F32, tag="mean_var")
             nc.vector.bn_aggr(out=mean_var[:], in_=stats[:])
+            seam_neg_mean = small.tile([P, 1], F32, tag="seam_neg_mean")
+            nc.vector.tensor_scalar_mul(out=seam_neg_mean[:], in0=mean_var[:, 0:1], scalar1=-1.0)
+            seam_var = small.tile([P, 1], F32, tag="seam_var")
+            nc.vector.tensor_scalar_add(out=seam_var[:], in0=mean_var[:, 1:2], scalar1=EPS)
+
             sums = small.tile([P, 2], F32, tag="sums")
             for j, n in enumerate(inner):
                 nc.scalar.activation(out=x_sb[:, n, :], in_=x1[:, n, :], func=ACT.Identity, accum_out=sums[:, j : j + 1])
@@ -249,30 +256,21 @@ def tile_swinmlpblock_pa_t_kernel(tc, h_pad, x, sw, sb, g2, b2, w1, bb1, out):
                     bias=neg_mean[:, j : j + 1],
                     accum_out=squares[:, j : j + 1],
                 )
-            return mean_var, neg_mean, squares
+            var = small.tile([P, 2], F32, tag="var")
+            nc.scalar.activation(out=var[:], in_=squares[:], func=ACT.Identity, scale=1.0 / C, bias=eps_col[:])
+            return seam_neg_mean, seam_var, neg_mean, var
 
-        def scale(x1, b, mean_var, neg_mean, squares):
+        def scale(x1, b, seam_neg_mean, seam_var, neg_mean, var):
             seam, inner = 4 + b, (2 * b, 2 * b + 1)
-            seam_scalars = small.tile([P, 2], F32, tag="seam_scalars")
-            nc.gpsimd.tensor_scalar(
-                out=seam_scalars[:, 0:1], in0=mean_var[:, 0:1], scalar1=-1.0, scalar2=0.0, op0=ALU.mult, op1=ALU.add
-            )
-            nc.gpsimd.tensor_scalar(
-                out=seam_scalars[:, 1:2], in0=mean_var[:, 1:2], scalar1=1.0, scalar2=EPS, op0=ALU.mult, op1=ALU.add
-            )
-            nc.gpsimd.tensor_tensor(
-                out=seam_scalars[:, 1:2], in0=seam_scalars[:, 1:2], in1=minus_half[:, 0:1], op=ALU.pow
-            )
+            seam_rstd = small.tile([P, 1], F32, tag="seam_rstd")
+            nc.gpsimd.tensor_tensor(out=seam_rstd[:], in0=seam_var[:], in1=minus_half[:, 0:1], op=ALU.pow)
             rstd = small.tile([P, 2], F32, tag="rstd")
-            nc.gpsimd.tensor_scalar(
-                out=rstd[:], in0=squares[:], scalar1=1.0 / C, scalar2=EPS, op0=ALU.mult, op1=ALU.add
-            )
-            nc.gpsimd.tensor_tensor(out=rstd[:], in0=rstd[:], in1=minus_half[:], op=ALU.pow)
+            nc.gpsimd.tensor_tensor(out=rstd[:], in0=var[:], in1=minus_half[:], op=ALU.pow)
             nc.vector.tensor_scalar(
                 out=x1[:, seam, :],
                 in0=x1[:, seam, :],
-                scalar1=seam_scalars[:, 0:1],
-                scalar2=seam_scalars[:, 1:2],
+                scalar1=seam_neg_mean[:],
+                scalar2=seam_rstd[:],
                 op0=ALU.add,
                 op1=ALU.mult,
             )

@@ -97,13 +97,6 @@ def tile_swinmlpblock_pa_t_kernel(tc, h_pad, x, sw, sb, g2, b2, w1, bb1, out):
                         nc.sync.dma_start(out=x_sb[p0 + ROWS - 1 : p1 : ROWS, n, :], in_=x_view[b, w0:w1_, y_last, :])
             return x_sb
 
-        sw_nat = x1_pool.tile([P, 2, HEADS, WS * WS], BF16, tag="x1")
-        sw_view = sw.rearrange("h (t p) j -> t p h j", t=2)
-        nc.sync.dma_start(out=sw_nat[:, 0], in_=sw_view[0])
-        windows = load_windows(1)
-        x_next = load_x(WS - CROP, WS - CROP + ROWS - 1)
-        nc.sync.dma_start(out=sw_nat[:, 1], in_=sw_view[1])
-
         vec_rows = act_pool.tile([P, P], BF16, tag="act")
         nc.vector.memset(vec_rows[:].bitcast(I32), 0)
         nc.scalar.dma_start(out=vec_rows[0:BLOCKS, :], in_=g2.rearrange("(k p) -> k p", p=P))
@@ -111,8 +104,14 @@ def tile_swinmlpblock_pa_t_kernel(tc, h_pad, x, sw, sb, g2, b2, w1, bb1, out):
         sb_rows = act_pool.tile([P, 2 * P], BF16, tag="act")
         nc.vector.memset(sb_rows[:].bitcast(I32), 0)
         nc.scalar.dma_start(out=sb_rows[0:HEADS, :], in_=sb)
-        bias_bc = const.tile([P, HID], BF16)
-        nc.scalar.dma_start(out=bias_bc[:], in_=bb1.partition_broadcast(P))
+
+        sw_nat = x1_pool.tile([P, 2, HEADS, WS * WS], BF16, tag="x1")
+        sw_view = sw.rearrange("h (t p) j -> t p h j", t=2)
+        nc.sync.dma_start(out=sw_nat[:, 0], in_=sw_view[0])
+        windows = load_windows(1)
+        x_next = load_x(WS - CROP, WS - CROP + ROWS - 1)
+        nc.sync.dma_start(out=sw_nat[:, 1], in_=sw_view[1])
+
         sb_perm = act_pool.tile([P, 3, WS, ROWS], BF16, tag="act")
         nc.vector.tensor_copy(
             out=sb_perm[:, 0:2, :, :], in_=sb_rows[:].rearrange("p (t r c) -> p t c r", t=2, r=ROWS, c=WS)
@@ -182,9 +181,11 @@ def tile_swinmlpblock_pa_t_kernel(tc, h_pad, x, sw, sb, g2, b2, w1, bb1, out):
 
         w1_codes = const.tile([P, PASSES, HID], U32, align_bytes=64)
         w1_scales = const.tile([P, PASSES, HID], U8, align_bytes=64)
+        bias_bc = const.tile([P, HID], BF16)
 
         def prepare_w1():
             w1_view = w1.rearrange("(g t p) n -> g p t n", g=PASSES, t=PACK)
+            nc.sync.dma_start(out=bias_bc[:], in_=bb1.partition_broadcast(P))
             for g in range(PASSES):
                 raw = plane_pool.tile([P, PACK, HID], BF16, tag="planes")
                 nc.sync.dma_start(out=raw[:], in_=w1_view[g])
@@ -264,9 +265,7 @@ def tile_swinmlpblock_pa_t_kernel(tc, h_pad, x, sw, sb, g2, b2, w1, bb1, out):
             seam, inner = 4 + b, (2 * b, 2 * b + 1)
             seam_rstd = small.tile([P, 1], F32, tag="seam_rstd")
             nc.gpsimd.tensor_tensor(out=seam_rstd[:], in0=seam_var[:], in1=minus_half[:, 0:1], op=ALU.pow)
-            rstd = small.tile([P, 2], F32, tag="rstd")
-            nc.gpsimd.tensor_tensor(out=rstd[:], in0=var[:], in1=minus_half[:], op=ALU.pow)
-            nc.vector.tensor_scalar(
+            nc.gpsimd.tensor_scalar(
                 out=x1[:, seam, :],
                 in0=x1[:, seam, :],
                 scalar1=seam_neg_mean[:],
@@ -274,8 +273,10 @@ def tile_swinmlpblock_pa_t_kernel(tc, h_pad, x, sw, sb, g2, b2, w1, bb1, out):
                 op0=ALU.add,
                 op1=ALU.mult,
             )
+            rstd = small.tile([P, 2], F32, tag="rstd")
+            nc.gpsimd.tensor_tensor(out=rstd[:], in0=var[:], in1=minus_half[:], op=ALU.pow)
             for j, n in enumerate(inner):
-                nc.vector.tensor_scalar(
+                nc.gpsimd.tensor_scalar(
                     out=x1[:, n, :],
                     in0=x1[:, n, :],
                     scalar1=neg_mean[:, j : j + 1],
@@ -307,18 +308,16 @@ def tile_swinmlpblock_pa_t_kernel(tc, h_pad, x, sw, sb, g2, b2, w1, bb1, out):
             grouped = group_pool.tile([P, PASSES, STRIP, PACK], BF16, tag="grouped", align_bytes=64)
             codes = code_pool.tile([P, PASSES, STRIP], U32, tag="codes", align_bytes=64)
             scales = code_pool.tile([P, PASSES, STRIP], U8, tag="scales", align_bytes=64)
-            for g in range(PASSES):
-                src = planes[:, PACK * g : PACK * (g + 1), :].rearrange("p t (r w) -> p r w t", r=ROWS, w=MAP)
-                dst = grouped[:, g, :, :].rearrange("p (r w) t -> p r w t", r=ROWS, w=MAP)
-                nc.vector.tensor_copy(out=dst[:, :, 0 : MAP - SEAM, :], in_=src[:, :, SEAM:MAP, :])
-                nc.vector.tensor_copy(out=dst[:, :, MAP - SEAM : MAP, :], in_=src[:, :, 0:SEAM, :])
-            for g in range(PASSES):
-                for m in range(STRIP_TILES):
-                    nc.vector.quantize_mx(
-                        out=codes[:, g, P * m : P * (m + 1)].bitcast(FP8X4),
-                        scales=scales[:, g, P * m : P * (m + 1)],
-                        in_=grouped[:, g, P * m : P * (m + 1), :].rearrange("p a t -> p (a t)"),
-                    )
+            src = planes[:].rearrange("p (g t) (r w) -> p g r w t", g=PASSES, t=PACK, r=ROWS, w=MAP)
+            dst = grouped[:].rearrange("p g (r w) t -> p g r w t", r=ROWS, w=MAP)
+            nc.vector.tensor_copy(out=dst[:, :, :, 0 : MAP - SEAM, :], in_=src[:, :, :, SEAM:MAP, :])
+            nc.vector.tensor_copy(out=dst[:, :, :, MAP - SEAM : MAP, :], in_=src[:, :, :, 0:SEAM, :])
+            for w0, w1_ in ((0, 512), (512, PASSES * STRIP)):
+                nc.vector.quantize_mx(
+                    out=codes[:].rearrange("p g a -> p (g a)")[:, w0:w1_].bitcast(FP8X4),
+                    scales=scales[:].rearrange("p g a -> p (g a)")[:, w0:w1_],
+                    in_=grouped[:].rearrange("p g a t -> p (g a t)")[:, PACK * w0 : PACK * w1_],
+                )
             return codes, scales
 
         def project(codes, scales, b, y0, y_last):

@@ -64,6 +64,7 @@ def tile_swinmlpblock_pa_t_kernel(tc, h_pad, x, sw, sb, g2, b2, w1, bb1, out):
         nc.vector.tensor_copy(out=by_rows[:], in_=ident_f[:].rearrange("p (c r) -> p r c", c=WS, r=ROWS))
         minus_half = const.tile([P, 2], F32)
         nc.vector.memset(minus_half[:], -0.5)
+        unread = const.tile([P, C], BF16)
         eps_col = const.tile([P, 1], F32)
         nc.vector.memset(eps_col[:], EPS)
 
@@ -86,15 +87,20 @@ def tile_swinmlpblock_pa_t_kernel(tc, h_pad, x, sw, sb, g2, b2, w1, bb1, out):
 
         def load_x(y0, y_last):
             x_sb = x_pool.tile([P, UNITS, C], BF16, tag="x")
+            pieces = []
             for b in range(IMAGES):
-                pieces = [(0, P, 2 * b + wcol - 1, WS * wcol - CROP) for wcol in (1, 2)]
-                pieces.append((0, LEFT, 4 + b, MAP - SEAM))
-                pieces.append((LEFT, P, 4 + b, 0))
-                for p0, p1, n, w0 in pieces:
-                    w1_ = w0 + (p1 - p0) // ROWS
-                    nc.sync.dma_start(out=x_sb[p0:p1, n, :], in_=x_view[b, w0:w1_, y0 : y0 + ROWS, :])
-                    if y_last != y0 + ROWS - 1:
-                        nc.sync.dma_start(out=x_sb[p0 + ROWS - 1 : p1 : ROWS, n, :], in_=x_view[b, w0:w1_, y_last, :])
+                pieces.extend((b, 0, P, 2 * b + wcol - 1, WS * wcol - CROP) for wcol in (1, 2))
+                pieces.append((b, 0, LEFT, 4 + b, MAP - SEAM))
+                pieces.append((b, LEFT, P, 4 + b, 0))
+            for b, p0, p1, n, w0 in pieces:
+                nc.sync.dma_start(
+                    out=x_sb[p0:p1, n, :], in_=x_view[b, w0 : w0 + (p1 - p0) // ROWS, y0 : y0 + ROWS, :]
+                )
+            if y_last != y0 + ROWS - 1:
+                for b, p0, p1, n, w0 in pieces:
+                    nc.sync.dma_start(
+                        out=x_sb[p0 + ROWS - 1 : p1 : ROWS, n, :], in_=x_view[b, w0 : w0 + (p1 - p0) // ROWS, y_last, :]
+                    )
             return x_sb
 
         vec_rows = act_pool.tile([P, P], BF16, tag="act")
@@ -231,27 +237,25 @@ def tile_swinmlpblock_pa_t_kernel(tc, h_pad, x, sw, sb, g2, b2, w1, bb1, out):
                     op1=ALU.add,
                 )
 
-        def statistics(x1, x_sb, b):
+        def statistics(x1, b):
             seam, inner = 4 + b, (2 * b, 2 * b + 1)
             stats = small.tile([P, 2, 6], F32, tag="stats")
             for i in range(2):
                 nc.vector.bn_stats(out=stats[:, i, :], in_=x1[:, seam, 512 * i : 512 * (i + 1)])
             mean_var = small.tile([P, 2], F32, tag="mean_var")
             nc.vector.bn_aggr(out=mean_var[:], in_=stats[:])
-            seam_neg_mean = small.tile([P, 1], F32, tag="seam_neg_mean")
-            nc.vector.tensor_scalar_mul(out=seam_neg_mean[:], in0=mean_var[:, 0:1], scalar1=-1.0)
             seam_var = small.tile([P, 1], F32, tag="seam_var")
             nc.vector.tensor_scalar_add(out=seam_var[:], in0=mean_var[:, 1:2], scalar1=EPS)
 
             sums = small.tile([P, 2], F32, tag="sums")
             for j, n in enumerate(inner):
-                nc.scalar.activation(out=x_sb[:, n, :], in_=x1[:, n, :], func=ACT.Identity, accum_out=sums[:, j : j + 1])
+                nc.scalar.activation(out=unread[:], in_=x1[:, n, :], func=ACT.Identity, accum_out=sums[:, j : j + 1])
             neg_mean = small.tile([P, 2], F32, tag="neg_mean")
             nc.scalar.mul(out=neg_mean[:], in_=sums[:], mul=-1.0 / C)
             squares = small.tile([P, 2], F32, tag="squares")
             for j, n in enumerate(inner):
                 nc.scalar.activation(
-                    out=x_sb[:, n, :],
+                    out=unread[:],
                     in_=x1[:, n, :],
                     func=ACT.Square,
                     bias=neg_mean[:, j : j + 1],
@@ -259,24 +263,24 @@ def tile_swinmlpblock_pa_t_kernel(tc, h_pad, x, sw, sb, g2, b2, w1, bb1, out):
                 )
             var = small.tile([P, 2], F32, tag="var")
             nc.scalar.activation(out=var[:], in_=squares[:], func=ACT.Identity, scale=1.0 / C, bias=eps_col[:])
-            return seam_neg_mean, seam_var, neg_mean, var
+            return mean_var, seam_var, neg_mean, var
 
-        def scale(x1, b, seam_neg_mean, seam_var, neg_mean, var):
+        def scale(x1, b, mean_var, seam_var, neg_mean, var):
             seam, inner = 4 + b, (2 * b, 2 * b + 1)
             seam_rstd = small.tile([P, 1], F32, tag="seam_rstd")
             nc.gpsimd.tensor_tensor(out=seam_rstd[:], in0=seam_var[:], in1=minus_half[:, 0:1], op=ALU.pow)
-            nc.gpsimd.tensor_scalar(
-                out=x1[:, seam, :],
-                in0=x1[:, seam, :],
-                scalar1=seam_neg_mean[:],
-                scalar2=seam_rstd[:],
-                op0=ALU.add,
-                op1=ALU.mult,
-            )
             rstd = small.tile([P, 2], F32, tag="rstd")
             nc.gpsimd.tensor_tensor(out=rstd[:], in0=var[:], in1=minus_half[:], op=ALU.pow)
+            nc.vector.tensor_scalar(
+                out=x1[:, seam, :],
+                in0=x1[:, seam, :],
+                scalar1=mean_var[:, 0:1],
+                scalar2=seam_rstd[:],
+                op0=ALU.subtract,
+                op1=ALU.mult,
+            )
             for j, n in enumerate(inner):
-                nc.gpsimd.tensor_scalar(
+                nc.vector.tensor_scalar(
                     out=x1[:, n, :],
                     in0=x1[:, n, :],
                     scalar1=neg_mean[:, j : j + 1],
@@ -338,9 +342,9 @@ def tile_swinmlpblock_pa_t_kernel(tc, h_pad, x, sw, sb, g2, b2, w1, bb1, out):
                 nc.scalar.activation(out=act[:], in_=act[:], func=ACT.Gelu)
                 row = y0 * MAP + P * m
                 head = P if y_last == y0 + ROWS - 1 else min(P * (m + 1), STRIP - MAP) - P * m
-                nc.sync.dma_start(out=out[b, row : row + head, :], in_=act[0:head, :])
+                nc.scalar.dma_start(out=out[b, row : row + head, :], in_=act[0:head, :])
                 if head < P:
-                    nc.sync.dma_start(out=out[b, y_last * MAP : (y_last + 1) * MAP, :], in_=act[head:P, :])
+                    nc.scalar.dma_start(out=out[b, y_last * MAP : (y_last + 1) * MAP, :], in_=act[head:P, :])
 
         stages = []
         for wrow in (1, 2, 3):
@@ -368,6 +372,12 @@ def tile_swinmlpblock_pa_t_kernel(tc, h_pad, x, sw, sb, g2, b2, w1, bb1, out):
         with tc.manual_schedule():
             for fresh in range(n_stages + 2):
                 ripe, late = fresh - 1, fresh - 2
+                if live(fresh + 1):
+                    x_of[fresh + 1] = load_x(stages[fresh + 1][2], stages[fresh + 1][3])
+                if live(fresh + 2):
+                    for wrow in stages[fresh + 2][0]:
+                        if wrow not in held:
+                            held[wrow] = load_windows(wrow)
                 if live(fresh):
                     x1_of[fresh] = x1_pool.tile([P, UNITS, C], F32, tag="x1", name="x1")
 
@@ -377,18 +387,12 @@ def tile_swinmlpblock_pa_t_kernel(tc, h_pad, x, sw, sb, g2, b2, w1, bb1, out):
 
                 if live(ripe):
                     for b in range(IMAGES):
-                        stats_of[ripe, b] = statistics(x1_of[ripe], x_of[ripe], b)
+                        stats_of[ripe, b] = statistics(x1_of[ripe], b)
                 if live(late):
                     codes_of[late, 1] = pack(planes_of[late, 1])
                 mix_run(0)
                 if live(late):
                     project(codes_of[late, 1][0], codes_of[late, 1][1], 1, stages[late][2], stages[late][3])
-                if live(fresh + 1):
-                    x_of[fresh + 1] = load_x(stages[fresh + 1][2], stages[fresh + 1][3])
-                if live(fresh + 2):
-                    for wrow in stages[fresh + 2][0]:
-                        if wrow not in held:
-                            held[wrow] = load_windows(wrow)
                 if live(ripe):
                     scale(x1_of[ripe], 0, *stats_of[ripe, 0])
                 mix_run(1)

@@ -62,11 +62,8 @@ def tile_swinmlpblock_pa_t_kernel(tc, h_pad, x, sw, sb, g2, b2, w1, bb1, out):
         make_identity(nc, ident_b[:])
         by_rows = const.tile([P, ROWS, WS], F32)
         nc.vector.tensor_copy(out=by_rows[:], in_=ident_f[:].rearrange("p (c r) -> p r c", c=WS, r=ROWS))
-        minus_half = const.tile([P, 2], F32)
+        minus_half = const.tile([P, 3], F32)
         nc.vector.memset(minus_half[:], -0.5)
-        unread = const.tile([P, C], BF16)
-        eps_col = const.tile([P, 1], F32)
-        nc.vector.memset(eps_col[:], EPS)
 
         def load_windows(wrow):
             inner = win_pool.tile([P, 4, 2, C], BF16, tag="inner")
@@ -87,29 +84,16 @@ def tile_swinmlpblock_pa_t_kernel(tc, h_pad, x, sw, sb, g2, b2, w1, bb1, out):
 
         def load_x(y0, y_last):
             x_sb = x_pool.tile([P, UNITS, C], BF16, tag="x")
-            pieces = []
             for b in range(IMAGES):
-                pieces.extend((b, 0, P, 2 * b + wcol - 1, WS * wcol - CROP) for wcol in (1, 2))
-                pieces.append((b, 0, LEFT, 4 + b, MAP - SEAM))
-                pieces.append((b, LEFT, P, 4 + b, 0))
-            for b, p0, p1, n, w0 in pieces:
-                nc.sync.dma_start(
-                    out=x_sb[p0:p1, n, :], in_=x_view[b, w0 : w0 + (p1 - p0) // ROWS, y0 : y0 + ROWS, :]
-                )
-            if y_last != y0 + ROWS - 1:
-                for b, p0, p1, n, w0 in pieces:
-                    nc.sync.dma_start(
-                        out=x_sb[p0 + ROWS - 1 : p1 : ROWS, n, :], in_=x_view[b, w0 : w0 + (p1 - p0) // ROWS, y_last, :]
-                    )
+                pieces = [(0, P, 2 * b + wcol - 1, WS * wcol - CROP) for wcol in (1, 2)]
+                pieces.append((0, LEFT, 4 + b, MAP - SEAM))
+                pieces.append((LEFT, P, 4 + b, 0))
+                for p0, p1, n, w0 in pieces:
+                    w1_ = w0 + (p1 - p0) // ROWS
+                    nc.sync.dma_start(out=x_sb[p0:p1, n, :], in_=x_view[b, w0:w1_, y0 : y0 + ROWS, :])
+                    if y_last != y0 + ROWS - 1:
+                        nc.sync.dma_start(out=x_sb[p0 + ROWS - 1 : p1 : ROWS, n, :], in_=x_view[b, w0:w1_, y_last, :])
             return x_sb
-
-        vec_rows = act_pool.tile([P, P], BF16, tag="act")
-        nc.vector.memset(vec_rows[:].bitcast(I32), 0)
-        nc.scalar.dma_start(out=vec_rows[0:BLOCKS, :], in_=g2.rearrange("(k p) -> k p", p=P))
-        nc.scalar.dma_start(out=vec_rows[BLOCKS : 2 * BLOCKS, :], in_=b2.rearrange("(k p) -> k p", p=P))
-        sb_rows = act_pool.tile([P, 2 * P], BF16, tag="act")
-        nc.vector.memset(sb_rows[:].bitcast(I32), 0)
-        nc.scalar.dma_start(out=sb_rows[0:HEADS, :], in_=sb)
 
         sw_nat = x1_pool.tile([P, 2, HEADS, WS * WS], BF16, tag="x1")
         sw_view = sw.rearrange("h (t p) j -> t p h j", t=2)
@@ -118,6 +102,15 @@ def tile_swinmlpblock_pa_t_kernel(tc, h_pad, x, sw, sb, g2, b2, w1, bb1, out):
         x_next = load_x(WS - CROP, WS - CROP + ROWS - 1)
         nc.sync.dma_start(out=sw_nat[:, 1], in_=sw_view[1])
 
+        vec_rows = act_pool.tile([P, P], BF16, tag="act")
+        nc.vector.memset(vec_rows[:].bitcast(I32), 0)
+        nc.scalar.dma_start(out=vec_rows[0:BLOCKS, :], in_=g2.rearrange("(k p) -> k p", p=P))
+        nc.scalar.dma_start(out=vec_rows[BLOCKS : 2 * BLOCKS, :], in_=b2.rearrange("(k p) -> k p", p=P))
+        sb_rows = act_pool.tile([P, 2 * P], BF16, tag="act")
+        nc.vector.memset(sb_rows[:].bitcast(I32), 0)
+        nc.scalar.dma_start(out=sb_rows[0:HEADS, :], in_=sb)
+        bias_bc = const.tile([P, HID], BF16)
+        nc.scalar.dma_start(out=bias_bc[:], in_=bb1.partition_broadcast(P))
         sb_perm = act_pool.tile([P, 3, WS, ROWS], BF16, tag="act")
         nc.vector.tensor_copy(
             out=sb_perm[:, 0:2, :, :], in_=sb_rows[:].rearrange("p (t r c) -> p t c r", t=2, r=ROWS, c=WS)
@@ -175,23 +168,21 @@ def tile_swinmlpblock_pa_t_kernel(tc, h_pad, x, sw, sb, g2, b2, w1, bb1, out):
             return by_block(t, width)[:, :, m0:m1].rearrange("p n (c r) -> p n c r", r=ROWS)[:, :, :, 0:1]
 
         def prepare_seam_weights():
-            nc.vector.tensor_copy(out=first_rows(orphan, SPLIT, 0, LEFT), in_=first_rows(split[1], SPLIT, 0, LEFT))
-            nc.vector.tensor_copy(
+            nc.gpsimd.tensor_copy(out=first_rows(orphan, SPLIT, 0, LEFT), in_=first_rows(split[1], SPLIT, 0, LEFT))
+            nc.gpsimd.tensor_copy(
                 out=first_rows(orphan, SPLIT, 2 * LEFT, SPLIT), in_=first_rows(split[1], SPLIT, 2 * LEFT, SPLIT)
             )
-            nc.vector.memset(first_rows(whole[1], P, 0, P), 0.0)
-            nc.vector.memset(first_rows(split[1], SPLIT, 0, LEFT), 0.0)
-            nc.vector.memset(first_rows(split[1], SPLIT, 2 * LEFT, SPLIT), 0.0)
+            nc.gpsimd.memset(first_rows(whole[1], P, 0, P), 0.0)
+            nc.gpsimd.memset(first_rows(split[1], SPLIT, 0, LEFT), 0.0)
+            nc.gpsimd.memset(first_rows(split[1], SPLIT, 2 * LEFT, SPLIT), 0.0)
 
         prepare_weights(0)
 
         w1_codes = const.tile([P, PASSES, HID], U32, align_bytes=64)
         w1_scales = const.tile([P, PASSES, HID], U8, align_bytes=64)
-        bias_bc = const.tile([P, HID], BF16)
 
         def prepare_w1():
             w1_view = w1.rearrange("(g t p) n -> g p t n", g=PASSES, t=PACK)
-            nc.sync.dma_start(out=bias_bc[:], in_=bb1.partition_broadcast(P))
             for g in range(PASSES):
                 raw = plane_pool.tile([P, PACK, HID], BF16, tag="planes")
                 nc.sync.dma_start(out=raw[:], in_=w1_view[g])
@@ -237,49 +228,67 @@ def tile_swinmlpblock_pa_t_kernel(tc, h_pad, x, sw, sb, g2, b2, w1, bb1, out):
                     op1=ALU.add,
                 )
 
-        def statistics(x1, b):
-            seam, inner = 4 + b, (2 * b, 2 * b + 1)
-            stats = small.tile([P, 2, 6], F32, tag="stats")
-            for i in range(2):
-                nc.vector.bn_stats(out=stats[:, i, :], in_=x1[:, seam, 512 * i : 512 * (i + 1)])
-            mean_var = small.tile([P, 2], F32, tag="mean_var")
-            nc.vector.bn_aggr(out=mean_var[:], in_=stats[:])
-            seam_var = small.tile([P, 1], F32, tag="seam_var")
-            nc.vector.tensor_scalar_add(out=seam_var[:], in0=mean_var[:, 1:2], scalar1=EPS)
+        def shares(b):
+            if b == 0:
+                return (4, 0, 1), ()
+            return (5,), (2, 3)
 
-            sums = small.tile([P, 2], F32, tag="sums")
-            for j, n in enumerate(inner):
-                nc.scalar.activation(out=unread[:], in_=x1[:, n, :], func=ACT.Identity, accum_out=sums[:, j : j + 1])
-            neg_mean = small.tile([P, 2], F32, tag="neg_mean")
-            nc.scalar.mul(out=neg_mean[:], in_=sums[:], mul=-1.0 / C)
-            squares = small.tile([P, 2], F32, tag="squares")
-            for j, n in enumerate(inner):
-                nc.scalar.activation(
-                    out=unread[:],
-                    in_=x1[:, n, :],
-                    func=ACT.Square,
-                    bias=neg_mean[:, j : j + 1],
-                    accum_out=squares[:, j : j + 1],
-                )
-            var = small.tile([P, 2], F32, tag="var")
-            nc.scalar.activation(out=var[:], in_=squares[:], func=ACT.Identity, scale=1.0 / C, bias=eps_col[:])
-            return mean_var, seam_var, neg_mean, var
+        def statistics(x1, x_sb, b):
+            by_vector, by_scalar = shares(b)
+            mean_var = small.tile([P, 3, 2], F32, tag="mean_var")
+            for j, n in enumerate(by_vector):
+                stats = small.tile([P, 2, 6], F32, tag="stats")
+                for i in range(2):
+                    nc.vector.bn_stats(out=stats[:, i, :], in_=x1[:, n, 512 * i : 512 * (i + 1)])
+                nc.vector.bn_aggr(out=mean_var[:, j, :], in_=stats[:])
+            neg_mean, squares = None, None
+            if by_scalar:
+                neg_mean = small.tile([P, 2], F32, tag="neg_mean")
+                squares = small.tile([P, 2], F32, tag="squares")
+                sums = small.tile([P, 2], F32, tag="sums")
+                for j, n in enumerate(by_scalar):
+                    nc.scalar.activation(
+                        out=x_sb[:, n, :], in_=x1[:, n, :], func=ACT.Identity, accum_out=sums[:, j : j + 1]
+                    )
+                nc.scalar.mul(out=neg_mean[:], in_=sums[:], mul=-1.0 / C)
+                for j, n in enumerate(by_scalar):
+                    nc.scalar.activation(
+                        out=x_sb[:, n, :],
+                        in_=x1[:, n, :],
+                        func=ACT.Square,
+                        bias=neg_mean[:, j : j + 1],
+                        accum_out=squares[:, j : j + 1],
+                    )
+            return mean_var, neg_mean, squares
 
-        def scale(x1, b, mean_var, seam_var, neg_mean, var):
-            seam, inner = 4 + b, (2 * b, 2 * b + 1)
-            seam_rstd = small.tile([P, 1], F32, tag="seam_rstd")
-            nc.gpsimd.tensor_tensor(out=seam_rstd[:], in0=seam_var[:], in1=minus_half[:, 0:1], op=ALU.pow)
-            rstd = small.tile([P, 2], F32, tag="rstd")
-            nc.gpsimd.tensor_tensor(out=rstd[:], in0=var[:], in1=minus_half[:], op=ALU.pow)
-            nc.vector.tensor_scalar(
-                out=x1[:, seam, :],
-                in0=x1[:, seam, :],
-                scalar1=mean_var[:, 0:1],
-                scalar2=seam_rstd[:],
-                op0=ALU.subtract,
-                op1=ALU.mult,
+        def scale(x1, b, mean_var, neg_mean, squares):
+            by_vector, by_scalar = shares(b)
+            k = len(by_vector)
+            shift = small.tile([P, 3], F32, tag="shift")
+            gain = small.tile([P, 3], F32, tag="gain")
+            nc.gpsimd.tensor_scalar(
+                out=shift[:, 0:k], in0=mean_var[:, 0:k, 0], scalar1=-1.0, scalar2=0.0, op0=ALU.mult, op1=ALU.add
             )
-            for j, n in enumerate(inner):
+            nc.gpsimd.tensor_scalar(
+                out=gain[:, 0:k], in0=mean_var[:, 0:k, 1], scalar1=1.0, scalar2=EPS, op0=ALU.mult, op1=ALU.add
+            )
+            nc.gpsimd.tensor_tensor(out=gain[:, 0:k], in0=gain[:, 0:k], in1=minus_half[:, 0:k], op=ALU.pow)
+            if by_scalar:
+                rstd = small.tile([P, 2], F32, tag="rstd")
+                nc.gpsimd.tensor_scalar(
+                    out=rstd[:], in0=squares[:], scalar1=1.0 / C, scalar2=EPS, op0=ALU.mult, op1=ALU.add
+                )
+                nc.gpsimd.tensor_tensor(out=rstd[:], in0=rstd[:], in1=minus_half[:, 0:2], op=ALU.pow)
+            for j, n in enumerate(by_vector):
+                nc.vector.tensor_scalar(
+                    out=x1[:, n, :],
+                    in0=x1[:, n, :],
+                    scalar1=shift[:, j : j + 1],
+                    scalar2=gain[:, j : j + 1],
+                    op0=ALU.add,
+                    op1=ALU.mult,
+                )
+            for j, n in enumerate(by_scalar):
                 nc.vector.tensor_scalar(
                     out=x1[:, n, :],
                     in0=x1[:, n, :],
@@ -312,16 +321,18 @@ def tile_swinmlpblock_pa_t_kernel(tc, h_pad, x, sw, sb, g2, b2, w1, bb1, out):
             grouped = group_pool.tile([P, PASSES, STRIP, PACK], BF16, tag="grouped", align_bytes=64)
             codes = code_pool.tile([P, PASSES, STRIP], U32, tag="codes", align_bytes=64)
             scales = code_pool.tile([P, PASSES, STRIP], U8, tag="scales", align_bytes=64)
-            src = planes[:].rearrange("p (g t) (r w) -> p g r w t", g=PASSES, t=PACK, r=ROWS, w=MAP)
-            dst = grouped[:].rearrange("p g (r w) t -> p g r w t", r=ROWS, w=MAP)
-            nc.vector.tensor_copy(out=dst[:, :, :, 0 : MAP - SEAM, :], in_=src[:, :, :, SEAM:MAP, :])
-            nc.vector.tensor_copy(out=dst[:, :, :, MAP - SEAM : MAP, :], in_=src[:, :, :, 0:SEAM, :])
-            for w0, w1_ in ((0, 512), (512, PASSES * STRIP)):
-                nc.vector.quantize_mx(
-                    out=codes[:].rearrange("p g a -> p (g a)")[:, w0:w1_].bitcast(FP8X4),
-                    scales=scales[:].rearrange("p g a -> p (g a)")[:, w0:w1_],
-                    in_=grouped[:].rearrange("p g a t -> p (g a t)")[:, PACK * w0 : PACK * w1_],
-                )
+            for g in range(PASSES):
+                src = planes[:, PACK * g : PACK * (g + 1), :].rearrange("p t (r w) -> p r w t", r=ROWS, w=MAP)
+                dst = grouped[:, g, :, :].rearrange("p (r w) t -> p r w t", r=ROWS, w=MAP)
+                nc.vector.tensor_copy(out=dst[:, :, 0 : MAP - SEAM, :], in_=src[:, :, SEAM:MAP, :])
+                nc.vector.tensor_copy(out=dst[:, :, MAP - SEAM : MAP, :], in_=src[:, :, 0:SEAM, :])
+            for g in range(PASSES):
+                for m in range(STRIP_TILES):
+                    nc.vector.quantize_mx(
+                        out=codes[:, g, P * m : P * (m + 1)].bitcast(FP8X4),
+                        scales=scales[:, g, P * m : P * (m + 1)],
+                        in_=grouped[:, g, P * m : P * (m + 1), :].rearrange("p a t -> p (a t)"),
+                    )
             return codes, scales
 
         def project(codes, scales, b, y0, y_last):
@@ -372,12 +383,6 @@ def tile_swinmlpblock_pa_t_kernel(tc, h_pad, x, sw, sb, g2, b2, w1, bb1, out):
         with tc.manual_schedule():
             for fresh in range(n_stages + 2):
                 ripe, late = fresh - 1, fresh - 2
-                if live(fresh + 1):
-                    x_of[fresh + 1] = load_x(stages[fresh + 1][2], stages[fresh + 1][3])
-                if live(fresh + 2):
-                    for wrow in stages[fresh + 2][0]:
-                        if wrow not in held:
-                            held[wrow] = load_windows(wrow)
                 if live(fresh):
                     x1_of[fresh] = x1_pool.tile([P, UNITS, C], F32, tag="x1", name="x1")
 
@@ -387,7 +392,13 @@ def tile_swinmlpblock_pa_t_kernel(tc, h_pad, x, sw, sb, g2, b2, w1, bb1, out):
 
                 if live(ripe):
                     for b in range(IMAGES):
-                        stats_of[ripe, b] = statistics(x1_of[ripe], b)
+                        stats_of[ripe, b] = statistics(x1_of[ripe], x_of[ripe], b)
+                if live(fresh + 1):
+                    x_of[fresh + 1] = load_x(stages[fresh + 1][2], stages[fresh + 1][3])
+                if live(fresh + 2):
+                    for wrow in stages[fresh + 2][0]:
+                        if wrow not in held:
+                            held[wrow] = load_windows(wrow)
                 if live(late):
                     codes_of[late, 1] = pack(planes_of[late, 1])
                 mix_run(0)

from contextlib import ExitStack

import concourse.mybir as mybir
from concourse.masks import make_identity

F32 = mybir.dt.float32
BF16 = mybir.dt.bfloat16
I32 = mybir.dt.int32
U32 = mybir.dt.uint32
U8 = mybir.dt.uint8
FP8X4 = mybir.dt.float8_e4m3fn_x4
ALU = mybir.AluOpType
ACT = mybir.ActivationFunctionType

P = 128
IMAGES = 2
WS = 16
WINDOWS = 4
CROP = 9
MAP = 48
C = 1024
HEADS = 16
HD = C // HEADS
HID = 512
EPS = 1e-5
ROWS = 8
SEAM = CROP + MAP - WS * (WINDOWS - 1)
LEFT = SEAM * ROWS
UNITS = 6
PACK = 4
K_PASS = P * PACK
PASSES = C // K_PASS
BLOCKS = C // P
STRIP = ROWS * MAP
STRIP_TILES = STRIP // P
MARGIN = 16
SPLIT = LEFT + P

FLOPS = 2 * HEADS * (WS * WS) * (WS * WS) * (IMAGES * WINDOWS * WINDOWS * HD) + 2 * IMAGES * MAP * MAP * C * HID


def tile_swinmlpblock_pa_t_kernel(tc, h_pad, x, sw, sb, g2, b2, w1, bb1, out):
    nc = tc.nc
    with ExitStack() as ctx:
        const = ctx.enter_context(tc.tile_pool(name="const", bufs=1))
        win_pool = ctx.enter_context(tc.tile_pool(name="windows", bufs=2))
        x_pool = ctx.enter_context(tc.tile_pool(name="x", bufs=2))
        x1_pool = ctx.enter_context(tc.tile_pool(name="x1", bufs=2))
        small = ctx.enter_context(tc.tile_pool(name="small", bufs=4))
        plane_pool = ctx.enter_context(tc.tile_pool(name="planes", bufs=2))
        group_pool = ctx.enter_context(tc.tile_pool(name="grouped", bufs=2))
        code_pool = ctx.enter_context(tc.tile_pool(name="codes", bufs=2))
        act_pool = ctx.enter_context(tc.tile_pool(name="act", bufs=3))
        psum = ctx.enter_context(tc.psum_pool(name="psum", bufs=8))

        win_view = h_pad.rearrange("b (wr r) (wc k q) c -> b wr wc r k (q c)", r=WS, wc=WINDOWS, k=WS // 2, q=2)
        x_view = x.rearrange("b (y w) c -> b w y c", w=MAP)

        ident_f = const.tile([P, P], F32)
        make_identity(nc, ident_f[:])
        ident_b = const.tile([P, P], BF16)
        make_identity(nc, ident_b[:])
        by_rows = const.tile([P, ROWS, WS], F32)
        nc.vector.tensor_copy(out=by_rows[:], in_=ident_f[:].rearrange("p (c r) -> p r c", c=WS, r=ROWS))
        minus_half = const.tile([P, 3], F32)
        nc.vector.memset(minus_half[:], -0.5)

        def load_windows(wrow):
            inner = win_pool.tile([P, 4, 2, C], BF16, tag="inner")
            last = win_pool.tile([P, 2, 2, C], BF16, tag="last")
            first = win_pool.tile([P, 2, 2, C], BF16, tag="first")
            for b in range(IMAGES):
                for wcol in (1, 2):
                    nc.sync.dma_start(
                        out=inner[:, 2 * b + wcol - 1, :, :].rearrange("p q c -> p (q c)"),
                        in_=win_view[b, wrow, wcol],
                    )
            for b in range(IMAGES):
                nc.sync.dma_start(
                    out=last[:, b, :, :].rearrange("p q c -> p (q c)"), in_=win_view[b, wrow, WINDOWS - 1]
                )
                nc.sync.dma_start(out=first[:, b, :, :].rearrange("p q c -> p (q c)"), in_=win_view[b, wrow, 0])
            return inner, last, first

        def load_x(y0, y_last):
            x_sb = x_pool.tile([P, UNITS, C], BF16, tag="x")
            for b in range(IMAGES):
                pieces = [(0, P, 2 * b + wcol - 1, WS * wcol - CROP) for wcol in (1, 2)]
                pieces.append((0, LEFT, 4 + b, MAP - SEAM))
                pieces.append((LEFT, P, 4 + b, 0))
                for p0, p1, n, w0 in pieces:
                    w1_ = w0 + (p1 - p0) // ROWS
                    nc.sync.dma_start(out=x_sb[p0:p1, n, :], in_=x_view[b, w0:w1_, y0 : y0 + ROWS, :])
                    if y_last != y0 + ROWS - 1:
                        nc.sync.dma_start(out=x_sb[p0 + ROWS - 1 : p1 : ROWS, n, :], in_=x_view[b, w0:w1_, y_last, :])
            return x_sb

        sw_nat = x1_pool.tile([P, 2, HEADS, WS * WS], BF16, tag="x1")
        sw_view = sw.rearrange("h (t p) j -> t p h j", t=2)
        nc.sync.dma_start(out=sw_nat[:, 0], in_=sw_view[0])
        windows = load_windows(1)
        x_next = load_x(WS - CROP, WS - CROP + ROWS - 1)
        nc.sync.dma_start(out=sw_nat[:, 1], in_=sw_view[1])

        vec_rows = act_pool.tile([P, P], BF16, tag="act")
        nc.vector.memset(vec_rows[:].bitcast(I32), 0)
        nc.scalar.dma_start(out=vec_rows[0:BLOCKS, :], in_=g2.rearrange("(k p) -> k p", p=P))
        nc.scalar.dma_start(out=vec_rows[BLOCKS : 2 * BLOCKS, :], in_=b2.rearrange("(k p) -> k p", p=P))
        sb_rows = act_pool.tile([P, 2 * P], BF16, tag="act")
        nc.vector.memset(sb_rows[:].bitcast(I32), 0)
        nc.scalar.dma_start(out=sb_rows[0:HEADS, :], in_=sb)
        bias_bc = const.tile([P, HID], BF16)
        nc.scalar.dma_start(out=bias_bc[:], in_=bb1.partition_broadcast(P))
        sb_perm = act_pool.tile([P, 3, WS, ROWS], BF16, tag="act")
        nc.vector.tensor_copy(
            out=sb_perm[:, 0:2, :, :], in_=sb_rows[:].rearrange("p (t r c) -> p t c r", t=2, r=ROWS, c=WS)
        )
        nc.vector.tensor_copy(out=sb_perm[:, 2, :, 0 : ROWS - 1], in_=sb_perm[:, 1, :, 1:ROWS])
        nc.vector.tensor_copy(out=sb_perm[:, 2, :, ROWS - 1 : ROWS], in_=sb_perm[:, 1, :, 0:1])
        vec_ps = psum.tile([P, 4, P], BF16, tag="bank")
        nc.tensor.transpose(out=vec_ps[:, 0, :], in_=vec_rows[:], identity=ident_b[:])
        for i in range(3):
            nc.tensor.transpose(
                out=vec_ps[:, 1 + i, :], in_=sb_perm[:, i, :, :].rearrange("p c r -> p (c r)"), identity=ident_b[:]
            )
        gain_shift = const.tile([P, 2 * BLOCKS], F32)
        nc.vector.tensor_copy(out=gain_shift[:], in_=vec_ps[:, 0, 0 : 2 * BLOCKS])
        sb_col = const.tile([P, 3, HEADS], F32)
        nc.vector.tensor_copy(out=sb_col[:], in_=vec_ps[:, 1:4, 0:HEADS])

        n_blocks = 2 * HEADS
        whole = [const.tile([P, 2 * MARGIN + n_blocks * P], BF16, name="whole%d" % half) for half in range(2)]
        split = [const.tile([P, 2 * MARGIN + n_blocks * SPLIT], BF16, name="split%d" % half) for half in range(2)]
        orphan = const.tile([P, 2 * MARGIN + n_blocks * SPLIT], BF16)
        for t in whole:
            nc.vector.memset(t[:, 0:MARGIN].bitcast(I32), 0)
            nc.vector.memset(t[:, MARGIN + n_blocks * P :].bitcast(I32), 0)
        for t in split + [orphan]:
            nc.vector.memset(t[:].bitcast(I32), 0)

        def by_block(t, width):
            return t[:, MARGIN : MARGIN + n_blocks * width].rearrange("p (n m) -> p n m", m=width)

        def prepare_weights(half):
            for quad in range(HEADS // 4):
                sw_ps = psum.tile([P, 8, P], BF16, tag="bank")
                for i in range(8):
                    h, q = 4 * quad + i // 2, i % 2
                    nc.tensor.transpose(
                        out=sw_ps[:, i, :],
                        in_=sw_nat[:, half, h, :].rearrange("p (k q) -> p q k", q=2)[:, q, :],
                        identity=ident_b[:],
                    )
                dst = by_block(whole[half], P)[:, 8 * quad : 8 * (quad + 1), :].rearrange(
                    "p n (c r) -> p n c r", c=WS, r=ROWS
                )
                src = sw_ps[:].rearrange("p n (r c) -> p n c r", r=ROWS, c=WS)
                if quad % 2 == 0:
                    nc.vector.tensor_copy(out=dst, in_=src)
                else:
                    nc.scalar.copy(out=dst, in_=src)
            nc.vector.tensor_copy(out=by_block(split[half], SPLIT)[:, :, 0:LEFT], in_=by_block(whole[half], P)[:, :, 0:LEFT])
            nc.vector.tensor_copy(
                out=by_block(split[half], SPLIT)[:, :, 2 * LEFT : SPLIT], in_=by_block(whole[half], P)[:, :, LEFT:P]
            )

        def first_rows(t, width, m0, m1):
            return by_block(t, width)[:, :, m0:m1].rearrange("p n (c r) -> p n c r", r=ROWS)[:, :, :, 0:1]

        def prepare_seam_weights():
            nc.gpsimd.tensor_copy(out=first_rows(orphan, SPLIT, 0, LEFT), in_=first_rows(split[1], SPLIT, 0, LEFT))
            nc.gpsimd.tensor_copy(
                out=first_rows(orphan, SPLIT, 2 * LEFT, SPLIT), in_=first_rows(split[1], SPLIT, 2 * LEFT, SPLIT)
            )
            nc.gpsimd.memset(first_rows(whole[1], P, 0, P), 0.0)
            nc.gpsimd.memset(first_rows(split[1], SPLIT, 0, LEFT), 0.0)
            nc.gpsimd.memset(first_rows(split[1], SPLIT, 2 * LEFT, SPLIT), 0.0)

        prepare_weights(0)

        w1_codes = const.tile([P, PASSES, HID], U32, align_bytes=64)
        w1_scales = const.tile([P, PASSES, HID], U8, align_bytes=64)

        def prepare_w1():
            w1_view = w1.rearrange("(g t p) n -> g p t n", g=PASSES, t=PACK)
            for g in range(PASSES):
                raw = plane_pool.tile([P, PACK, HID], BF16, tag="planes")
                nc.sync.dma_start(out=raw[:], in_=w1_view[g])
                grouped = group_pool.tile([P, HID, PACK], BF16, tag="grouped", align_bytes=64)
                nc.vector.tensor_copy(out=grouped[:], in_=raw[:].rearrange("p t n -> p n t"))
                nc.vector.quantize_mx(
                    out=w1_codes[:, g, :].bitcast(FP8X4),
                    scales=w1_scales[:, g, :],
                    in_=grouped[:].rearrange("p n t -> p (n t)"),
                )

        def accumulate(acc, terms):
            for i, (weights, moving) in enumerate(terms):
                nc.tensor.matmul(out=acc, lhsT=weights, rhs=moving, start=(i == 0), stop=(i == len(terms) - 1))

        def mix(sources, sb_index, x_sb, x1, heads):
            for h in heads:
                cols = slice(HD * h, HD * (h + 1))
                inner_terms, seam_terms = [], []
                for (inner, last, first), whole_w, split_w, start in sources:
                    for q in range(2):
                        n = 2 * h + q
                        s0 = MARGIN + SPLIT * n + start
                        left_w = split_w[:, s0 : s0 + P]
                        right_w = split_w[:, s0 + LEFT : s0 + LEFT + P]
                        if whole_w is None:
                            inner_terms.append((left_w, inner[:, :, q, cols]))
                            inner_terms.append((right_w, inner[:, :, q, cols]))
                        else:
                            w0 = MARGIN + P * n + start
                            inner_terms.append((whole_w[:, w0 : w0 + P], inner[:, :, q, cols]))
                        seam_terms.append((left_w, last[:, :, q, cols]))
                        seam_terms.append((right_w, first[:, :, q, cols]))
                acc = psum.tile([P, UNITS, HD], F32, tag="bank")
                accumulate(acc[:, 0:4, :], inner_terms)
                accumulate(acc[:, 4:6, :], seam_terms)
                nc.vector.scalar_tensor_tensor(
                    out=x1[:, :, cols],
                    in0=acc[:],
                    scalar=sb_col[:, sb_index, h : h + 1],
                    in1=x_sb[:, :, cols],
                    op0=ALU.add,
                    op1=ALU.add,
                )

        def shares(b):
            if b == 0:
                return (4, 0, 1), ()
            return (5,), (2, 3)

        def statistics(x1, x_sb, b):
            by_vector, by_scalar = shares(b)
            mean_var = small.tile([P, 3, 2], F32, tag="mean_var")
            for j, n in enumerate(by_vector):
                stats = small.tile([P, 2, 6], F32, tag="stats")
                for i in range(2):
                    nc.vector.bn_stats(out=stats[:, i, :], in_=x1[:, n, 512 * i : 512 * (i + 1)])
                nc.vector.bn_aggr(out=mean_var[:, j, :], in_=stats[:])
            neg_mean, squares = None, None
            if by_scalar:
                neg_mean = small.tile([P, 2], F32, tag="neg_mean")
                squares = small.tile([P, 2], F32, tag="squares")
                sums = small.tile([P, 2], F32, tag="sums")
                for j, n in enumerate(by_scalar):
                    nc.scalar.activation(
                        out=x_sb[:, n, :], in_=x1[:, n, :], func=ACT.Identity, accum_out=sums[:, j : j + 1]
                    )
                nc.scalar.mul(out=neg_mean[:], in_=sums[:], mul=-1.0 / C)
                for j, n in enumerate(by_scalar):
                    nc.scalar.activation(
                        out=x_sb[:, n, :],
                        in_=x1[:, n, :],
                        func=ACT.Square,
                        bias=neg_mean[:, j : j + 1],
                        accum_out=squares[:, j : j + 1],
                    )
            return mean_var, neg_mean, squares

        def scale(x1, b, mean_var, neg_mean, squares):
            by_vector, by_scalar = shares(b)
            k = len(by_vector)
            shift = small.tile([P, 3], F32, tag="shift")
            gain = small.tile([P, 3], F32, tag="gain")
            nc.gpsimd.tensor_scalar(
                out=shift[:, 0:k], in0=mean_var[:, 0:k, 0], scalar1=-1.0, scalar2=0.0, op0=ALU.mult, op1=ALU.add
            )
            nc.gpsimd.tensor_scalar(
                out=gain[:, 0:k], in0=mean_var[:, 0:k, 1], scalar1=1.0, scalar2=EPS, op0=ALU.mult, op1=ALU.add
            )
            nc.gpsimd.tensor_tensor(out=gain[:, 0:k], in0=gain[:, 0:k], in1=minus_half[:, 0:k], op=ALU.pow)
            if by_scalar:
                rstd = small.tile([P, 2], F32, tag="rstd")
                nc.gpsimd.tensor_scalar(
                    out=rstd[:], in0=squares[:], scalar1=1.0 / C, scalar2=EPS, op0=ALU.mult, op1=ALU.add
                )
                nc.gpsimd.tensor_tensor(out=rstd[:], in0=rstd[:], in1=minus_half[:, 0:2], op=ALU.pow)
            for j, n in enumerate(by_vector):
                nc.vector.tensor_scalar(
                    out=x1[:, n, :],
                    in0=x1[:, n, :],
                    scalar1=shift[:, j : j + 1],
                    scalar2=gain[:, j : j + 1],
                    op0=ALU.add,
                    op1=ALU.mult,
                )
            for j, n in enumerate(by_scalar):
                nc.vector.tensor_scalar(
                    out=x1[:, n, :],
                    in0=x1[:, n, :],
                    scalar1=neg_mean[:, j : j + 1],
                    scalar2=rstd[:, j : j + 1],
                    op0=ALU.add,
                    op1=ALU.mult,
                )

        def flip(x1, b):
            planes = plane_pool.tile([P, BLOCKS, 3 * P], BF16, tag="planes")
            for k in range(BLOCKS):
                turned = psum.tile([P, ROWS, MAP], F32, tag="bank")
                for slot, n in enumerate((4 + b, 2 * b, 2 * b + 1)):
                    nc.tensor.transpose(
                        out=turned[:, :, WS * slot : WS * (slot + 1)],
                        in_=x1[:, n, P * k : P * (k + 1)],
                        identity=by_rows[:],
                    )
                nc.scalar.activation(
                    out=planes[:, k, :],
                    in_=turned[:].rearrange("p r w -> p (r w)"),
                    func=ACT.Identity,
                    scale=gain_shift[:, k : k + 1],
                    bias=gain_shift[:, BLOCKS + k : BLOCKS + k + 1],
                )
            return planes

        def pack(planes):
            grouped = group_pool.tile([P, PASSES, STRIP, PACK], BF16, tag="grouped", align_bytes=64)
            codes = code_pool.tile([P, PASSES, STRIP], U32, tag="codes", align_bytes=64)
            scales = code_pool.tile([P, PASSES, STRIP], U8, tag="scales", align_bytes=64)
            for g in range(PASSES):
                src = planes[:, PACK * g : PACK * (g + 1), :].rearrange("p t (r w) -> p r w t", r=ROWS, w=MAP)
                dst = grouped[:, g, :, :].rearrange("p (r w) t -> p r w t", r=ROWS, w=MAP)
                nc.vector.tensor_copy(out=dst[:, :, 0 : MAP - SEAM, :], in_=src[:, :, SEAM:MAP, :])
                nc.vector.tensor_copy(out=dst[:, :, MAP - SEAM : MAP, :], in_=src[:, :, 0:SEAM, :])
            for g in range(PASSES):
                for m in range(STRIP_TILES):
                    nc.vector.quantize_mx(
                        out=codes[:, g, P * m : P * (m + 1)].bitcast(FP8X4),
                        scales=scales[:, g, P * m : P * (m + 1)],
                        in_=grouped[:, g, P * m : P * (m + 1), :].rearrange("p a t -> p (a t)"),
                    )
            return codes, scales

        def project(codes, scales, b, y0, y_last):
            for m in range(STRIP_TILES):
                acc = psum.tile([P, HID], F32, tag="bank")
                for g in range(PASSES):
                    nc.tensor.matmul_mx(
                        out=acc[:],
                        lhsT=codes[:, g, P * m : P * (m + 1)].bitcast(FP8X4),
                        lhsT_scale=scales[:, g, P * m : P * (m + 1)],
                        rhs=w1_codes[:, g, :].bitcast(FP8X4),
                        rhs_scale=w1_scales[:, g, :],
                        start=(g == 0),
                        stop=(g == PASSES - 1),
                    )
                act = act_pool.tile([P, HID], F32, tag="act")
                nc.vector.tensor_tensor(out=act[:], in0=acc[:], in1=bias_bc[:], op=ALU.add)
                nc.scalar.activation(out=act[:], in_=act[:], func=ACT.Gelu)
                row = y0 * MAP + P * m
                head = P if y_last == y0 + ROWS - 1 else min(P * (m + 1), STRIP - MAP) - P * m
                nc.scalar.dma_start(out=out[b, row : row + head, :], in_=act[0:head, :])
                if head < P:
                    nc.scalar.dma_start(out=out[b, y_last * MAP : (y_last + 1) * MAP, :], in_=act[head:P, :])

        stages = []
        for wrow in (1, 2, 3):
            for half in range(2):
                y0 = WS * wrow + ROWS * half - CROP
                if y0 + ROWS <= MAP:
                    stages.append(((wrow,), half, y0, y0 + ROWS - 1))
        stages.append(((0, WINDOWS - 1), 2, 0, MAP - 1))

        last_second_half = max(i for i, stage in enumerate(stages) if stage[1] == 1)
        n_stages = len(stages)

        def live(i):
            return 0 <= i < n_stages

        def sources_of(i):
            wrows, half = stages[i][0], stages[i][1]
            if half < 2:
                return [(held[wrows[0]], whole[half], split[half], 0)]
            return [(held[wrows[0]], whole[1], split[1], 1), (held[wrows[1]], None, orphan, 1 - ROWS)]

        held = {1: windows}
        x_of, x1_of, stats_of, planes_of, codes_of = {0: x_next}, {}, {}, {}, {}
        runs = (range(0, 8), range(8, 12), range(12, 14), range(14, 16))
        with tc.manual_schedule():
            for fresh in range(n_stages + 2):
                ripe, late = fresh - 1, fresh - 2
                if live(fresh):
                    x1_of[fresh] = x1_pool.tile([P, UNITS, C], F32, tag="x1", name="x1")

                def mix_run(k):
                    if live(fresh):
                        mix(sources_of(fresh), stages[fresh][1], x_of[fresh], x1_of[fresh], runs[k])

                if live(ripe):
                    for b in range(IMAGES):
                        stats_of[ripe, b] = statistics(x1_of[ripe], x_of[ripe], b)
                if live(fresh + 1):
                    x_of[fresh + 1] = load_x(stages[fresh + 1][2], stages[fresh + 1][3])
                if live(fresh + 2):
                    for wrow in stages[fresh + 2][0]:
                        if wrow not in held:
                            held[wrow] = load_windows(wrow)
                if live(late):
                    codes_of[late, 1] = pack(planes_of[late, 1])
                mix_run(0)
                if live(late):
                    project(codes_of[late, 1][0], codes_of[late, 1][1], 1, stages[late][2], stages[late][3])
                if live(ripe):
                    scale(x1_of[ripe], 0, *stats_of[ripe, 0])
                mix_run(1)
                if live(ripe):
                    planes_of[ripe, 0] = flip(x1_of[ripe], 0)
                    scale(x1_of[ripe], 1, *stats_of[ripe, 1])
                mix_run(2)
                if live(ripe):
                    planes_of[ripe, 1] = flip(x1_of[ripe], 1)
                    codes_of[ripe, 0] = pack(planes_of[ripe, 0])
                mix_run(3)
                if live(ripe):
                    project(codes_of[ripe, 0][0], codes_of[ripe, 0][1], 0, stages[ripe][2], stages[ripe][3])
                if fresh == 0:
                    prepare_weights(1)
                    prepare_w1()
                if fresh == last_second_half:
                    prepare_seam_weights()
